import numpy as np
import ml_dtypes


def mxq(x, axis, fmt="e4m3"):
    dtype, down = {"e4m3": (ml_dtypes.float8_e4m3fn, 7), "e5m2": (ml_dtypes.float8_e5m2, 14)}[fmt]
    v = np.moveaxis(np.asarray(x, np.float32).astype(ml_dtypes.bfloat16).astype(np.float64), axis, -1)
    blocks = v.reshape(v.shape[:-1] + (-1, 32))
    amax = np.abs(blocks).max(-1, keepdims=True)
    byte = np.maximum(np.where(amax > 0, np.frexp(amax)[1] - 1 + 127, 0) - down, 1)
    scale = np.exp2(byte - 127.0)
    codes = (blocks / scale).astype(np.float32).astype(dtype).astype(np.float64)
    return np.moveaxis((codes * scale).reshape(v.shape), -1, axis)


WIDE = False


def mx_kscale(k):
    if not WIDE:
        return np.ones(k)
    levels = np.array([10, -10, 5, -5, 0])
    a = np.random.permutation(np.resize(levels, k // 512 * 4)).reshape(k // 512, 4)
    idx = np.arange(k)
    return np.exp2(a[idx // 512, idx % 128 // 32])


BF16 = ml_dtypes.bfloat16


def bf(x):
    return np.asarray(x, np.float32).astype(BF16)


def f64(x):
    return np.asarray(x).astype(np.float64)


B, I, C, L, O, KW, P = 1, 512, 4, 128, 128, 3, 1


def setup_inputs():
    s = mx_kscale(I)
    return {"x": bf(np.random.standard_normal((B, I, C, L)) * s[None, :, None, None]),
            "time_tensor": bf(np.random.uniform(0.0, 1.0, (B, C, L))),
            "weights": bf(np.random.standard_normal((O, I, C, KW)) / np.sqrt(I * KW) / s[None, :, None, None])}


def reference(x, time_tensor, weights):
    xq = mxq(f64(x).transpose(0, 2, 1, 3), 2, "e4m3")
    wt = f64(weights).transpose(3, 2, 0, 1)
    tp = np.pad(f64(time_tensor), ((0, 0), (0, 0), (P, P)))
    Lw = L + 2 * P - KW + 1
    conv = np.zeros((B, C, O, Lw))
    for j in range(KW):
        y = mxq(wt[j], 2, "e4m3") @ xq
        conv = conv + np.pad(y, ((0, 0), (0, 0), (0, 0), (P, P)))[..., j:j + Lw]
    conv = np.transpose(conv, (0, 2, 1, 3))
    conv = np.pad(conv, ((0, 0), (0, 0), (0, 0), (P, P)))
    out = conv * tp[:, None, :, :]
    return out[..., P:-P]

@@ -1,0 +1,108 @@
+from contextlib import ExitStack
+
+import concourse.mybir as mybir
+
+BF16 = mybir.dt.bfloat16
+F32 = mybir.dt.float32
+U32 = mybir.dt.uint32
+U8 = mybir.dt.uint8
+FP8X4 = mybir.dt.float8_e4m3fn_x4
+
+P = 128
+PACK = 4
+I, C, L, O, KW = 512, 4, 128, 128, 3
+CK = C * KW
+HALF = L // 2
+BLOCKS = KW + 1
+O_CHUNK = 32
+CK_RUN = 4
+
+FLOPS = 2 * O * I * C * KW * L
+
+
+def tile_timeawareconv1d_s_kernel(tc, x, time_tensor, weights, out):
+    nc = tc.nc
+    assert I == P * PACK
+
+    x_rows = x.rearrange("b (p j) c l -> p (b j) (c l)", j=PACK)
+    w_runs = weights.rearrange("o (p j) c k -> p o (j c k)", j=PACK)
+    time_row = time_tensor.rearrange("b c l -> (b c l)")
+    out_rows = out.rearrange("b o c l -> o (b c) l")
+
+    with ExitStack() as ctx:
+        keep = ctx.enter_context(tc.tile_pool(name="keep", bufs=1))
+        psum = ctx.enter_context(tc.psum_pool(name="psum", bufs=C))
+
+        x_raw = keep.tile([P, PACK, C, L], BF16)
+        nc.sync.dma_start(out=x_raw[:].rearrange("p j c l -> p j (c l)"), in_=x_rows)
+        time_all = keep.tile([P, C, L], BF16)
+        nc.scalar.dma_start(
+            out=time_all[:].rearrange("p c l -> p (c l)"), in_=time_row.partition_broadcast(P)
+        )
+        w_raw = []
+        for h in range(O // O_CHUNK):
+            chunk = keep.tile([P, O_CHUNK, PACK, CK], BF16, name="w_raw%d" % h)
+            nc.sync.dma_start(
+                out=chunk[:].rearrange("p o j q -> p o (j q)"),
+                in_=w_runs[:, h * O_CHUNK : (h + 1) * O_CHUNK, :],
+            )
+            w_raw.append(chunk)
+
+        x_grouped = keep.tile([P, C, BLOCKS, HALF, PACK], BF16, align_bytes=64)
+        x_codes = keep.tile([P, C, BLOCKS * HALF], U32, align_bytes=64)
+        x_scales = keep.tile([P, C, BLOCKS * HALF], U8, align_bytes=64)
+        x_by_parity = x_raw[:].rearrange("p j c (n e) -> p e c n j", e=2)
+        nc.vector.tensor_copy(out=x_grouped[:, :, 1, :, :], in_=x_by_parity[:, 0])
+        nc.vector.tensor_copy(out=x_grouped[:, :, 2, :, :], in_=x_by_parity[:, 1])
+        nc.vector.memset(x_grouped[:, :, 0, 0, :], 0.0)
+        nc.vector.tensor_copy(out=x_grouped[:, :, 0, 1:HALF, :], in_=x_grouped[:, :, 2, 0 : HALF - 1, :])
+        nc.vector.tensor_copy(out=x_grouped[:, :, 3, 0 : HALF - 1, :], in_=x_grouped[:, :, 1, 1:HALF, :])
+        nc.vector.memset(x_grouped[:, :, 3, HALF - 1, :], 0.0)
+        nc.vector.quantize_mx(
+            out=x_codes[:].rearrange("p c w -> p (c w)").bitcast(FP8X4),
+            scales=x_scales[:].rearrange("p c w -> p (c w)"),
+            in_=x_grouped[:].rearrange("p c s n j -> p (c s n j)"),
+        )
+
+        w_grouped = keep.tile([P, CK, O, PACK], BF16, align_bytes=64)
+        w_codes = keep.tile([P, CK, O], U32, align_bytes=64)
+        w_scales = keep.tile([P, CK, O], U8, align_bytes=64)
+        for h in range(O // O_CHUNK):
+            o_cols = slice(h * O_CHUNK, (h + 1) * O_CHUNK)
+            for g in range(CK // CK_RUN):
+                run = slice(g * CK_RUN, (g + 1) * CK_RUN)
+                copy = nc.scalar.copy if g == 2 else nc.vector.tensor_copy
+                copy(
+                    out=w_grouped[:, run, o_cols, :].rearrange("p q o j -> p o j q"),
+                    in_=w_raw[h][:, :, :, run],
+                )
+        for g in range(CK // CK_RUN):
+            run = slice(g * CK_RUN, (g + 1) * CK_RUN)
+            nc.vector.quantize_mx(
+                out=w_codes[:, run, :].rearrange("p q o -> p (q o)").bitcast(FP8X4),
+                scales=w_scales[:, run, :].rearrange("p q o -> p (q o)"),
+                in_=w_grouped[:, run, :, :].rearrange("p q o j -> p (q o j)"),
+            )
+
+        out_sb = keep.tile([P, C, L], F32)
+        for c in range(C):
+            acc = psum.tile([P, L], F32)
+            for k in range(KW):
+                window = slice(k * HALF, k * HALF + L)
+                nc.tensor.matmul_mx(
+                    out=acc[:],
+                    lhsT=w_codes[:, c * KW + k, :].bitcast(FP8X4),
+                    lhsT_scale=w_scales[:, c * KW + k, :],
+                    rhs=x_codes[:, c, window].bitcast(FP8X4),
+                    rhs_scale=x_scales[:, c, window],
+                    start=(k == 0),
+                    stop=(k == KW - 1),
+                )
+            nc.vector.tensor_tensor(
+                out=out_sb[:, c, :].rearrange("p (n e) -> p n e", e=2),
+                in0=acc[:].rearrange("p (e n) -> p n e", e=2),
+                in1=time_all[:, c, :].rearrange("p (n e) -> p n e", e=2),
+                op=mybir.AluOpType.mult,
+            )
+            if c % 2 == 1:
+                nc.sync.dma_start(out=out_rows[:, c - 1 : c + 1, :], in_=out_sb[:, c - 1 : c + 1, :])

@@ -1,6 +1,7 @@
 from contextlib import ExitStack
 
 import concourse.mybir as mybir
+from concourse.masks import make_identity
 
 BF16 = mybir.dt.bfloat16
 F32 = mybir.dt.float32
@@ -12,46 +13,51 @@ P = 128
 PACK = 4
 I, C, L, O, KW = 512, 4, 128, 128, 3
 CK = C * KW
+PAIRS = CK // 2
 HALF = L // 2
 BLOCKS = KW + 1
-O_CHUNK = 32
-CK_RUN = 4
+ROUND = 3
 
 FLOPS = 2 * O * I * C * KW * L
 
 
 def tile_timeawareconv1d_s_kernel(tc, x, time_tensor, weights, out):
     nc = tc.nc
-    assert I == P * PACK
+    assert I == P * PACK and O == P
 
-    x_rows = x.rearrange("b (p j) c l -> p (b j) (c l)", j=PACK)
-    w_runs = weights.rearrange("o (p j) c k -> p o (j c k)", j=PACK)
+    x_rows = x.rearrange("b (t p) c l -> p (b t) (c l)", p=P)
+    w_rows = weights.rearrange("o (t i) c k -> t o (i c k)", t=PACK)
     time_row = time_tensor.rearrange("b c l -> (b c l)")
     out_rows = out.rearrange("b o c l -> o (b c) l")
 
     with ExitStack() as ctx:
         keep = ctx.enter_context(tc.tile_pool(name="keep", bufs=1))
-        psum = ctx.enter_context(tc.psum_pool(name="psum", bufs=C))
+        psum_w = ctx.enter_context(tc.psum_pool(name="psum_w", bufs=PAIRS))
+        psum_acc = ctx.enter_context(tc.psum_pool(name="psum_acc", bufs=2))
 
+        identity = keep.tile([P, P], F32)
+        make_identity(nc, identity[:])
+
+        w_raw = [keep.tile([P, P, CK], BF16, name="w_raw%d" % t) for t in range(PACK)]
         x_raw = keep.tile([P, PACK, C, L], BF16)
-        nc.sync.dma_start(out=x_raw[:].rearrange("p j c l -> p j (c l)"), in_=x_rows)
         time_all = keep.tile([P, C, L], BF16)
-        nc.scalar.dma_start(
+        for t in range(PACK):
+            nc.sync.dma_start(out=w_raw[t][:].rearrange("o i q -> o (i q)"), in_=w_rows[t])
+            if t == 1:
+                nc.sync.dma_start(out=x_raw[:].rearrange("p t c l -> p t (c l)"), in_=x_rows)
+        nc.sync.dma_start(
             out=time_all[:].rearrange("p c l -> p (c l)"), in_=time_row.partition_broadcast(P)
         )
-        w_raw = []
-        for h in range(O // O_CHUNK):
-            chunk = keep.tile([P, O_CHUNK, PACK, CK], BF16, name="w_raw%d" % h)
-            nc.sync.dma_start(
-                out=chunk[:].rearrange("p o j q -> p o (j q)"),
-                in_=w_runs[:, h * O_CHUNK : (h + 1) * O_CHUNK, :],
-            )
-            w_raw.append(chunk)
+
+        w_banks = [psum_w.tile([P, PACK, O], F32, name="w_bank%d" % w, tag="w_bank") for w in range(PAIRS)]
+        for t in range(PACK):
+            for w in range(PAIRS):
+                nc.tensor.transpose(w_banks[w][:, t, :], w_raw[t][:].bitcast(F32)[:, :, w], identity[:])
 
         x_grouped = keep.tile([P, C, BLOCKS, HALF, PACK], BF16, align_bytes=64)
         x_codes = keep.tile([P, C, BLOCKS * HALF], U32, align_bytes=64)
         x_scales = keep.tile([P, C, BLOCKS * HALF], U8, align_bytes=64)
-        x_by_parity = x_raw[:].rearrange("p j c (n e) -> p e c n j", e=2)
+        x_by_parity = x_raw[:].rearrange("p t c (n e) -> p e c n t", e=2)
         nc.vector.tensor_copy(out=x_grouped[:, :, 1, :, :], in_=x_by_parity[:, 0])
         nc.vector.tensor_copy(out=x_grouped[:, :, 2, :, :], in_=x_by_parity[:, 1])
         nc.vector.memset(x_grouped[:, :, 0, 0, :], 0.0)
@@ -61,48 +67,57 @@ def tile_timeawareconv1d_s_kernel(tc, x, time_tensor, weights, out):
         nc.vector.quantize_mx(
             out=x_codes[:].rearrange("p c w -> p (c w)").bitcast(FP8X4),
             scales=x_scales[:].rearrange("p c w -> p (c w)"),
-            in_=x_grouped[:].rearrange("p c s n j -> p (c s n j)"),
+            in_=x_grouped[:].rearrange("p c s n t -> p (c s n t)"),
         )
 
         w_grouped = keep.tile([P, CK, O, PACK], BF16, align_bytes=64)
         w_codes = keep.tile([P, CK, O], U32, align_bytes=64)
         w_scales = keep.tile([P, CK, O], U8, align_bytes=64)
-        for h in range(O // O_CHUNK):
-            o_cols = slice(h * O_CHUNK, (h + 1) * O_CHUNK)
-            for g in range(CK // CK_RUN):
-                run = slice(g * CK_RUN, (g + 1) * CK_RUN)
-                copy = nc.scalar.copy if g == 2 else nc.vector.tensor_copy
-                copy(
-                    out=w_grouped[:, run, o_cols, :].rearrange("p q o j -> p o j q"),
-                    in_=w_raw[h][:, :, :, run],
-                )
-        for g in range(CK // CK_RUN):
-            run = slice(g * CK_RUN, (g + 1) * CK_RUN)
-            nc.vector.quantize_mx(
-                out=w_codes[:, run, :].rearrange("p q o -> p (q o)").bitcast(FP8X4),
-                scales=w_scales[:, run, :].rearrange("p q o -> p (q o)"),
-                in_=w_grouped[:, run, :, :].rearrange("p q o j -> p (q o j)"),
-            )
-
         out_sb = keep.tile([P, C, L], F32)
-        for c in range(C):
-            acc = psum.tile([P, L], F32)
-            for k in range(KW):
-                window = slice(k * HALF, k * HALF + L)
-                nc.tensor.matmul_mx(
-                    out=acc[:],
-                    lhsT=w_codes[:, c * KW + k, :].bitcast(FP8X4),
-                    lhsT_scale=w_scales[:, c * KW + k, :],
-                    rhs=x_codes[:, c, window].bitcast(FP8X4),
-                    rhs_scale=x_scales[:, c, window],
-                    start=(k == 0),
-                    stop=(k == KW - 1),
+
+        def copy_out(r):
+            for w in (r * ROUND + 2, r * ROUND, r * ROUND + 1):
+                engine_copy = nc.vector.tensor_copy if w % ROUND == 2 else nc.scalar.copy
+                engine_copy(
+                    out=w_grouped[:, 2 * w : 2 * w + 2, :, :],
+                    in_=w_banks[w][:].bitcast(BF16).rearrange("p t (o e) -> p e o t", e=2),
                 )
+
+        def quantise(r):
+            for w in range(r * ROUND, (r + 1) * ROUND):
+                both = slice(2 * w, 2 * w + 2)
+                nc.vector.quantize_mx(
+                    out=w_codes[:, both, :].rearrange("p q o -> p (q o)").bitcast(FP8X4),
+                    scales=w_scales[:, both, :].rearrange("p q o -> p (q o)"),
+                    in_=w_grouped[:, both, :, :].rearrange("p q o t -> p (q o t)"),
+                )
+
+        def finish(r):
+            channels = slice(2 * r, 2 * r + 2)
+            acc = psum_acc.tile([P, 2, L], F32)
+            for c in (2 * r, 2 * r + 1):
+                for k in range(KW):
+                    window = slice(k * HALF, k * HALF + L)
+                    nc.tensor.matmul_mx(
+                        out=acc[:, c % 2, :],
+                        lhsT=w_codes[:, c * KW + k, :].bitcast(FP8X4),
+                        lhsT_scale=w_scales[:, c * KW + k, :],
+                        rhs=x_codes[:, c, window].bitcast(FP8X4),
+                        rhs_scale=x_scales[:, c, window],
+                        start=(k == 0),
+                        stop=(k == KW - 1),
+                    )
             nc.vector.tensor_tensor(
-                out=out_sb[:, c, :].rearrange("p (n e) -> p n e", e=2),
-                in0=acc[:].rearrange("p (e n) -> p n e", e=2),
-                in1=time_all[:, c, :].rearrange("p (n e) -> p n e", e=2),
+                out=out_sb[:, channels, :].rearrange("p c (n e) -> p c n e", e=2),
+                in0=acc[:].rearrange("p c (e n) -> p c n e", e=2),
+                in1=time_all[:, channels, :].rearrange("p c (n e) -> p c n e", e=2),
                 op=mybir.AluOpType.mult,
             )
-            if c % 2 == 1:
-                nc.sync.dma_start(out=out_rows[:, c - 1 : c + 1, :], in_=out_sb[:, c - 1 : c + 1, :])
+            nc.sync.dma_start(out=out_rows[:, channels, :], in_=out_sb[:, channels, :])
+
+        copy_out(0)
+        quantise(0)
+        copy_out(1)
+        finish(0)
+        quantise(1)
+        finish(1)

@@ -27,7 +27,7 @@ def tile_timeawareconv1d_s_kernel(tc, x, time_tensor, weights, out):
 
     x_rows = x.rearrange("b (t p) c l -> p (b t) (c l)", p=P)
     w_rows = weights.rearrange("o (t i) c k -> t o (i c k)", t=PACK)
-    time_row = time_tensor.rearrange("b c l -> (b c l)")
+    time_row = time_tensor.rearrange("b c l -> b (c l)")
     out_rows = out.rearrange("b o c l -> o (b c) l")
 
     with ExitStack() as ctx:
@@ -38,16 +38,24 @@ def tile_timeawareconv1d_s_kernel(tc, x, time_tensor, weights, out):
         identity = keep.tile([P, P], F32)
         make_identity(nc, identity[:])
 
+        ones = keep.tile([P, P], BF16)
+        nc.vector.memset(ones[:], 1.0)
+        time_in_row0 = keep.tile([P, C * L], BF16)
+        nc.vector.memset(time_in_row0[:], 0.0)
+        nc.scalar.dma_start(out=time_in_row0[0:1, :], in_=time_row)
+        time_bank = psum_acc.tile([P, C, L], F32, tag="acc")
+        nc.tensor.matmul(
+            out=time_bank[:].rearrange("p c l -> p (c l)"), lhsT=ones[:], rhs=time_in_row0[:], start=True, stop=True
+        )
+        time_all = keep.tile([P, C, L], F32)
+        nc.scalar.copy(out=time_all[:], in_=time_bank[:])
+
         w_raw = [keep.tile([P, P, CK], BF16, name="w_raw%d" % t) for t in range(PACK)]
         x_raw = keep.tile([P, PACK, C, L], BF16)
-        time_all = keep.tile([P, C, L], BF16)
         for t in range(PACK):
             nc.sync.dma_start(out=w_raw[t][:].rearrange("o i q -> o (i q)"), in_=w_rows[t])
             if t == 1:
                 nc.sync.dma_start(out=x_raw[:].rearrange("p t c l -> p t (c l)"), in_=x_rows)
-        nc.sync.dma_start(
-            out=time_all[:].rearrange("p c l -> p (c l)"), in_=time_row.partition_broadcast(P)
-        )
 
         w_banks = [psum_w.tile([P, PACK, O], F32, name="w_bank%d" % w, tag="w_bank") for w in range(PAIRS)]
         for t in range(PACK):
@@ -94,7 +102,7 @@ def tile_timeawareconv1d_s_kernel(tc, x, time_tensor, weights, out):
 
         def finish(r):
             channels = slice(2 * r, 2 * r + 2)
-            acc = psum_acc.tile([P, 2, L], F32)
+            acc = psum_acc.tile([P, 2, L], F32, tag="acc")
             for c in (2 * r, 2 * r + 1):
                 for k in range(KW):
                     window = slice(k * HALF, k * HALF + L)

@@ -43,12 +43,6 @@ def tile_timeawareconv1d_s_kernel(tc, x, time_tensor, weights, out):
         time_in_row0 = keep.tile([P, C * L], BF16)
         nc.vector.memset(time_in_row0[:], 0.0)
         nc.scalar.dma_start(out=time_in_row0[0:1, :], in_=time_row)
-        time_bank = psum_acc.tile([P, C, L], F32, tag="acc")
-        nc.tensor.matmul(
-            out=time_bank[:].rearrange("p c l -> p (c l)"), lhsT=ones[:], rhs=time_in_row0[:], start=True, stop=True
-        )
-        time_all = keep.tile([P, C, L], F32)
-        nc.scalar.copy(out=time_all[:], in_=time_bank[:])
 
         w_raw = [keep.tile([P, P, CK], BF16, name="w_raw%d" % t) for t in range(PACK)]
         x_raw = keep.tile([P, PACK, C, L], BF16)
@@ -58,9 +52,21 @@ def tile_timeawareconv1d_s_kernel(tc, x, time_tensor, weights, out):
                 nc.sync.dma_start(out=x_raw[:].rearrange("p t c l -> p t (c l)"), in_=x_rows)
 
         w_banks = [psum_w.tile([P, PACK, O], F32, name="w_bank%d" % w, tag="w_bank") for w in range(PAIRS)]
-        for t in range(PACK):
+        time_all = keep.tile([P, C, L], F32)
+        for half in range(2):
             for w in range(PAIRS):
-                nc.tensor.transpose(w_banks[w][:, t, :], w_raw[t][:].bitcast(F32)[:, :, w], identity[:])
+                for t in (2 * half, 2 * half + 1):
+                    nc.tensor.transpose(w_banks[w][:, t, :], w_raw[t][:].bitcast(F32)[:, :, w], identity[:])
+            if half == 0:
+                time_bank = psum_acc.tile([P, C, L], F32, tag="acc")
+                nc.tensor.matmul(
+                    out=time_bank[:].rearrange("p c l -> p (c l)"),
+                    lhsT=ones[:],
+                    rhs=time_in_row0[:],
+                    start=True,
+                    stop=True,
+                )
+                nc.scalar.copy(out=time_all[:], in_=time_bank[:])
 
         x_grouped = keep.tile([P, C, BLOCKS, HALF, PACK], BF16, align_bytes=64)
         x_codes = keep.tile([P, C, BLOCKS * HALF], U32, align_bytes=64)

from contextlib import ExitStack

import concourse.mybir as mybir
from concourse.masks import make_identity

BF16 = mybir.dt.bfloat16
F32 = mybir.dt.float32
U32 = mybir.dt.uint32
U8 = mybir.dt.uint8
FP8X4 = mybir.dt.float8_e4m3fn_x4

P = 128
PACK = 4
I, C, L, O, KW = 512, 4, 128, 128, 3
CK = C * KW
PAIRS = CK // 2
HALF = L // 2
BLOCKS = KW + 1
ROUND = 3

FLOPS = 2 * O * I * C * KW * L


def tile_timeawareconv1d_s_kernel(tc, x, time_tensor, weights, out):
    nc = tc.nc
    assert I == P * PACK and O == P

    x_rows = x.rearrange("b (t p) c l -> p (b t) (c l)", p=P)
    w_rows = weights.rearrange("o (t i) c k -> t o (i c k)", t=PACK)
    time_row = time_tensor.rearrange("b c l -> b (c l)")
    out_rows = out.rearrange("b o c l -> o (b c) l")

    with ExitStack() as ctx:
        keep = ctx.enter_context(tc.tile_pool(name="keep", bufs=1))
        psum_w = ctx.enter_context(tc.psum_pool(name="psum_w", bufs=PAIRS))
        psum_acc = ctx.enter_context(tc.psum_pool(name="psum_acc", bufs=2))

        identity = keep.tile([P, P], F32)
        make_identity(nc, identity[:])

        ones = keep.tile([P, P], BF16)
        nc.vector.memset(ones[:], 1.0)
        time_in_row0 = keep.tile([P, C * L], BF16)
        nc.vector.memset(time_in_row0[:], 0.0)
        nc.scalar.dma_start(out=time_in_row0[0:1, :], in_=time_row)

        w_raw = [keep.tile([P, P, CK], BF16, name="w_raw%d" % t) for t in range(PACK)]
        x_raw = keep.tile([P, PACK, C, L], BF16)
        for t in range(PACK):
            nc.sync.dma_start(out=w_raw[t][:].rearrange("o i q -> o (i q)"), in_=w_rows[t])
            if t == 1:
                nc.sync.dma_start(out=x_raw[:].rearrange("p t c l -> p t (c l)"), in_=x_rows)

        w_banks = [psum_w.tile([P, PACK, O], F32, name="w_bank%d" % w, tag="w_bank") for w in range(PAIRS)]
        time_all = keep.tile([P, C, L], F32)
        for half in range(2):
            for w in range(PAIRS):
                for t in (2 * half, 2 * half + 1):
                    nc.tensor.transpose(w_banks[w][:, t, :], w_raw[t][:].bitcast(F32)[:, :, w], identity[:])
            if half == 0:
                time_bank = psum_acc.tile([P, C, L], F32, tag="acc")
                nc.tensor.matmul(
                    out=time_bank[:].rearrange("p c l -> p (c l)"),
                    lhsT=ones[:],
                    rhs=time_in_row0[:],
                    start=True,
                    stop=True,
                )
                nc.scalar.copy(out=time_all[:], in_=time_bank[:])

        x_grouped = keep.tile([P, C, BLOCKS, HALF, PACK], BF16, align_bytes=64)
        x_codes = keep.tile([P, C, BLOCKS * HALF], U32, align_bytes=64)
        x_scales = keep.tile([P, C, BLOCKS * HALF], U8, align_bytes=64)
        x_by_parity = x_raw[:].rearrange("p t c (n e) -> p e c n t", e=2)
        nc.vector.tensor_copy(out=x_grouped[:, :, 1, :, :], in_=x_by_parity[:, 0])
        nc.vector.tensor_copy(out=x_grouped[:, :, 2, :, :], in_=x_by_parity[:, 1])
        nc.vector.memset(x_grouped[:, :, 0, 0, :], 0.0)
        nc.vector.tensor_copy(out=x_grouped[:, :, 0, 1:HALF, :], in_=x_grouped[:, :, 2, 0 : HALF - 1, :])
        nc.vector.tensor_copy(out=x_grouped[:, :, 3, 0 : HALF - 1, :], in_=x_grouped[:, :, 1, 1:HALF, :])
        nc.vector.memset(x_grouped[:, :, 3, HALF - 1, :], 0.0)
        nc.vector.quantize_mx(
            out=x_codes[:].rearrange("p c w -> p (c w)").bitcast(FP8X4),
            scales=x_scales[:].rearrange("p c w -> p (c w)"),
            in_=x_grouped[:].rearrange("p c s n t -> p (c s n t)"),
        )

        w_grouped = keep.tile([P, CK, O, PACK], BF16, align_bytes=64)
        w_codes = keep.tile([P, CK, O], U32, align_bytes=64)
        w_scales = keep.tile([P, CK, O], U8, align_bytes=64)
        out_sb = keep.tile([P, C, L], F32)

        def copy_out(r):
            for w in (r * ROUND + 2, r * ROUND, r * ROUND + 1):
                engine_copy = nc.vector.tensor_copy if w % ROUND == 2 else nc.scalar.copy
                engine_copy(
                    out=w_grouped[:, 2 * w : 2 * w + 2, :, :],
                    in_=w_banks[w][:].bitcast(BF16).rearrange("p t (o e) -> p e o t", e=2),
                )

        def quantise(r):
            for w in range(r * ROUND, (r + 1) * ROUND):
                both = slice(2 * w, 2 * w + 2)
                nc.vector.quantize_mx(
                    out=w_codes[:, both, :].rearrange("p q o -> p (q o)").bitcast(FP8X4),
                    scales=w_scales[:, both, :].rearrange("p q o -> p (q o)"),
                    in_=w_grouped[:, both, :, :].rearrange("p q o t -> p (q o t)"),
                )

        def finish(r):
            channels = slice(2 * r, 2 * r + 2)
            acc = psum_acc.tile([P, 2, L], F32, tag="acc")
            for c in (2 * r, 2 * r + 1):
                for k in range(KW):
                    window = slice(k * HALF, k * HALF + L)
                    nc.tensor.matmul_mx(
                        out=acc[:, c % 2, :],
                        lhsT=w_codes[:, c * KW + k, :].bitcast(FP8X4),
                        lhsT_scale=w_scales[:, c * KW + k, :],
                        rhs=x_codes[:, c, window].bitcast(FP8X4),
                        rhs_scale=x_scales[:, c, window],
                        start=(k == 0),
                        stop=(k == KW - 1),
                    )
            nc.vector.tensor_tensor(
                out=out_sb[:, channels, :].rearrange("p c (n e) -> p c n e", e=2),
                in0=acc[:].rearrange("p c (e n) -> p c n e", e=2),
                in1=time_all[:, channels, :].rearrange("p c (n e) -> p c n e", e=2),
                op=mybir.AluOpType.mult,
            )
            nc.sync.dma_start(out=out_rows[:, channels, :], in_=out_sb[:, channels, :])

        copy_out(0)
        quantise(0)
        copy_out(1)
        finish(0)
        quantise(1)
        finish(1)
